import numpy as np
import ml_dtypes


def mxq(x, axis, fmt="e4m3"):
    dtype, down = {"e4m3": (ml_dtypes.float8_e4m3fn, 7), "e5m2": (ml_dtypes.float8_e5m2, 14)}[fmt]
    v = np.moveaxis(np.asarray(x, np.float32).astype(ml_dtypes.bfloat16).astype(np.float64), axis, -1)
    blocks = v.reshape(v.shape[:-1] + (-1, 32))
    amax = np.abs(blocks).max(-1, keepdims=True)
    byte = np.maximum(np.where(amax > 0, np.frexp(amax)[1] - 1 + 127, 0) - down, 1)
    scale = np.exp2(byte - 127.0)
    codes = (blocks / scale).astype(np.float32).astype(dtype).astype(np.float64)
    return np.moveaxis((codes * scale).reshape(v.shape), -1, axis)


WIDE = False


def mx_kscale(k):
    if not WIDE:
        return np.ones(k)
    levels = np.array([10, -10, 5, -5, 0])
    a = np.random.permutation(np.resize(levels, k // 512 * 4)).reshape(k // 512, 4)
    idx = np.arange(k)
    return np.exp2(a[idx // 512, idx % 128 // 32])


BF16 = ml_dtypes.bfloat16


def bf(x):
    return np.asarray(x, np.float32).astype(BF16)


def f64(x):
    return np.asarray(x).astype(np.float64)


N, V, DIM, DY, HID, MLP_HID = 16, 512, 256, 512, 128, 1024


def setup_inputs():
    s = mx_kscale(DY)
    return {"q": bf(np.random.standard_normal((N, V, HID)) * 1.4),
            "k": bf(np.random.standard_normal((N, V, HID)) * 1.4),
            "y": bf(np.random.standard_normal((N, V, DY)) * s),
            "Wv": bf(np.random.standard_normal((DY, DIM)) * 2.0 / np.sqrt(DY) / s[:, None]),
            "x": bf(np.random.standard_normal((N, V, DIM)))}


def reference(q, k, y, Wv, x):
    v = mxq(f64(y), 2, "e4m3") @ mxq(f64(Wv), 0, "e4m3")
    s = f64(q) @ f64(k).transpose(0, 2, 1) * HID ** (-0.5)
    e = np.exp(s - s.max(-1, keepdims=True))
    return f64(x) + (mxq(e, 2, "e4m3") @ mxq(v, 1, "e4m3")) / e.sum(-1, keepdims=True)

@@ -1,0 +1,295 @@
+from contextlib import ExitStack
+
+import concourse.mybir as mybir
+from concourse.masks import make_identity
+
+F32 = mybir.dt.float32
+BF16 = mybir.dt.bfloat16
+U32 = mybir.dt.uint32
+U8 = mybir.dt.uint8
+FP8X4 = mybir.dt.float8_e4m3fn_x4
+ACT = mybir.ActivationFunctionType
+ALU = mybir.AluOpType
+AXIS = mybir.AxisListType
+
+BATCHES, ROWS, DIM, DY, HID = 16, 512, 256, 512, 128
+P = 128
+PACK = 4
+PAIRS = 2 * BATCHES
+SCALE = HID ** -0.5
+FLOPS = 2 * BATCHES * ROWS * (DY * DIM + ROWS * HID + ROWS * DIM)
+
+
+def tile_block_pa_t_kernel(tc, q, k, y, Wv, x, out):
+    nc = tc.nc
+    with ExitStack() as ctx:
+        const = ctx.enter_context(tc.tile_pool(name="const", bufs=1))
+        loads = ctx.enter_context(tc.tile_pool(name="loads", bufs=4))
+        work = ctx.enter_context(tc.tile_pool(name="work", bufs=3))
+        small = ctx.enter_context(tc.tile_pool(name="small", bufs=4))
+        psum_s = ctx.enter_context(tc.psum_pool(name="psum_s", bufs=4))
+        psum_tr = ctx.enter_context(tc.psum_pool(name="psum_tr", bufs=2))
+        psum_mx = ctx.enter_context(tc.psum_pool(name="psum_mx", bufs=2))
+        ctx.enter_context(tc.manual_schedule())
+
+        live = {}
+
+        def load_batch(b):
+            if not 0 <= b < BATCHES:
+                return
+            for name, src, bufs in (("q", q, 4), ("k", k, 4), ("y", y, 4), ("x", x, 6)):
+                width = PACK * src.shape[2]
+                rows = loads.tile([P, width], BF16, name=name + "_sb", tag=name, bufs=bufs)
+                nc.sync.dma_start(out=rows[:], in_=src[b].rearrange("(p t) c -> p (t c)", t=PACK))
+                live[name, b] = rows
+
+        load_batch(0)
+        w_rows = const.tile([P, PACK, DIM], BF16, name="w_rows")
+        for u in range(2):
+            nc.sync.dma_start(
+                out=w_rows[:, 2 * u : 2 * u + 2, :],
+                in_=Wv[256 * u : 256 * (u + 1), :].rearrange("(p e) c -> p e c", e=2),
+            )
+        load_batch(1)
+
+        warm = const.tile([P, 1], F32, name="warm")
+        nc.vector.memset(warm[:], 0.0)
+        nc.scalar.activation(out=warm[:], in_=warm[:], func=ACT.Exp)
+
+        ident_bf16 = const.tile([P, P], BF16, name="ident_bf16")
+        make_identity(nc, ident_bf16[:])
+        ident_f32 = const.tile([P, P], F32, name="ident_f32")
+        make_identity(nc, ident_f32[:])
+
+        w_grouped = const.tile([P, DIM, PACK], BF16, name="w_grouped", align_bytes=64)
+        w_codes = const.tile([P, DIM], U32, name="w_codes", align_bytes=64)
+        w_scales = const.tile([P, DIM], U8, name="w_scales", align_bytes=64)
+        nc.vector.tensor_copy(out=w_grouped[:], in_=w_rows[:].rearrange("p t c -> p c t"))
+        nc.vector.quantize_mx(
+            out=w_codes[:].bitcast(FP8X4),
+            scales=w_scales[:],
+            in_=w_grouped[:].rearrange("p c t -> p (c t)"),
+        )
+
+        def transpose_qk(b):
+            if not 0 <= b < BATCHES:
+                return
+            qk_ps = psum_mx.tile([P, 2 * ROWS], BF16, name="qk_ps", tag="mx")
+            for m, name in enumerate(("q", "k")):
+                for t in range(PACK):
+                    nc.tensor.transpose(
+                        qk_ps[:, m * ROWS + t * P : m * ROWS + (t + 1) * P],
+                        live[name, b][:, t * HID : (t + 1) * HID],
+                        ident_bf16[:],
+                    )
+            qk_t = work.tile([P, 2 * ROWS], BF16, name="qk_t", tag="qk_t")
+            nc.scalar.copy(out=qk_t[:], in_=qk_ps[:])
+            live["qk_t", b] = qk_t
+
+        def transpose_y(b, half):
+            if not 0 <= b < BATCHES:
+                return
+            y_words = live["y", b][:].bitcast(F32)
+            yt_ps = psum_tr.tile([P, 2, 2, P], F32, name="yt_ps", tag="tr")
+            for a in range(2):
+                for u in range(2):
+                    first = (2 * half + a) * (DY // 2) + u * P
+                    nc.tensor.transpose(yt_ps[:, a, u, :], y_words[:, first : first + P], ident_f32[:])
+            live["yt_ps", b, half] = yt_ps
+
+        def group_y(b, half):
+            if not 0 <= b < BATCHES:
+                return
+            if half == 0:
+                live["y_grouped", b] = work.tile(
+                    [P, ROWS * PACK], BF16, name="y_grouped", tag="y_grouped", align_bytes=64
+                )
+            words = live["y_grouped", b][:].bitcast(F32).rearrange("p (a m u) -> p a m u", a=PACK, u=2)
+            nc.scalar.copy(
+                out=words[:, 2 * half : 2 * half + 2, :, :],
+                in_=live["yt_ps", b, half][:].rearrange("p a u m -> p a m u"),
+            )
+
+        def quantise_y(b):
+            if not 0 <= b < BATCHES:
+                return
+            y_codes = work.tile([P, ROWS], U32, name="y_codes", tag="y_codes", align_bytes=64)
+            y_scales = work.tile([P, ROWS], U8, name="y_scales", tag="y_scales", align_bytes=64)
+            nc.vector.quantize_mx(out=y_codes[:].bitcast(FP8X4), scales=y_scales[:], in_=live["y_grouped", b][:])
+            live["y_codes", b] = y_codes
+            live["y_scales", b] = y_scales
+
+        def project_values(b, half):
+            if not 0 <= b < BATCHES:
+                return
+            v_ps = psum_mx.tile([P, PACK, P], F32, name="v_ps", tag="mx")
+            cols = slice(half * P, (half + 1) * P)
+            for t in range(PACK):
+                keys = slice(t * P, (t + 1) * P)
+                nc.tensor.matmul_mx(
+                    out=v_ps[:, t, :],
+                    lhsT=live["y_codes", b][:, keys].bitcast(FP8X4),
+                    lhsT_scale=live["y_scales", b][:, keys],
+                    rhs=w_codes[:, cols].bitcast(FP8X4),
+                    rhs_scale=w_scales[:, cols],
+                    start=True,
+                    stop=True,
+                )
+            live["v_ps", b, half] = v_ps
+
+        def group_v(b, half):
+            if not 0 <= b < BATCHES:
+                return
+            if half == 0:
+                live["v_grouped", b] = work.tile(
+                    [P, DIM, PACK], BF16, name="v_grouped", tag="v_grouped", align_bytes=64
+                )
+            nc.vector.tensor_copy(
+                out=live["v_grouped", b][:, half * P : (half + 1) * P, :],
+                in_=live["v_ps", b, half][:].rearrange("p t c -> p c t"),
+            )
+
+        def quantise_v(b):
+            if not 0 <= b < BATCHES:
+                return
+            v_codes = work.tile([P, DIM], U32, name="v_codes", tag="v_codes", align_bytes=64)
+            v_scales = work.tile([P, DIM], U8, name="v_scales", tag="v_scales", align_bytes=64)
+            nc.vector.quantize_mx(
+                out=v_codes[:].bitcast(FP8X4),
+                scales=v_scales[:],
+                in_=live["v_grouped", b][:].rearrange("p c t -> p (c t)"),
+            )
+            live["v_codes", b] = v_codes
+            live["v_scales", b] = v_scales
+
+        def scores(g):
+            if not 0 <= g < PAIRS:
+                return
+            qk_t = live["qk_t", g // 2]
+            for i in range(2):
+                tile_i = 2 * (g % 2) + i
+                s_ps = psum_s.tile([P, ROWS], F32, name="s_ps", tag="s")
+                nc.tensor.matmul(
+                    out=s_ps[:],
+                    lhsT=qk_t[:, tile_i * P : (tile_i + 1) * P],
+                    rhs=qk_t[:, ROWS : 2 * ROWS],
+                    start=True,
+                    stop=True,
+                )
+                live["s_ps", g, i] = s_ps
+
+        def row_maxima(g):
+            if not 0 <= g < PAIRS:
+                return
+            top = small.tile([P, 2], F32, name="top", tag="top")
+            for i in range(2):
+                nc.vector.tensor_reduce(out=top[:, i : i + 1], in_=live["s_ps", g, i][:], axis=AXIS.X, op=ALU.max)
+            shift = small.tile([P, 2], F32, name="shift", tag="shift")
+            nc.gpsimd.tensor_scalar(out=shift[:], in0=top[:], scalar1=-SCALE, scalar2=0.0, op0=ALU.mult, op1=ALU.add)
+            live["shift", g] = shift
+
+        def exponentials(g):
+            if not 0 <= g < PAIRS:
+                return
+            e_sb = work.tile([P, 2, ROWS], BF16, name="e_sb", tag="e_sb")
+            e_sum = small.tile([P, 2], F32, name="e_sum", tag="e_sum")
+            for i in range(2):
+                nc.scalar.activation(
+                    out=e_sb[:, i, :],
+                    in_=live["s_ps", g, i][:],
+                    func=ACT.Exp,
+                    bias=live["shift", g][:, i : i + 1],
+                    scale=SCALE,
+                    accum_out=e_sum[:, i : i + 1],
+                )
+            live["e_sb", g] = e_sb
+            live["e_sum", g] = e_sum
+
+        def transpose_e(g):
+            if not 0 <= g < PAIRS:
+                return
+            et_ps = psum_tr.tile([P, 2, PACK, P], BF16, name="et_ps", tag="tr")
+            for i in range(2):
+                for t in range(PACK):
+                    nc.tensor.transpose(et_ps[:, i, t, :], live["e_sb", g][:, i, t * P : (t + 1) * P], ident_bf16[:])
+            live["et_ps", g] = et_ps
+
+        def group_e(g):
+            if not 0 <= g < PAIRS:
+                return
+            e_grouped = work.tile([P, 2, P, PACK], BF16, name="e_grouped", tag="e_grouped", align_bytes=64)
+            nc.scalar.copy(out=e_grouped[:], in_=live["et_ps", g][:].rearrange("p i t r -> p i r t"))
+            live["e_grouped", g] = e_grouped
+
+        def quantise_e(g):
+            if not 0 <= g < PAIRS:
+                return
+            e_codes = work.tile([P, 2 * P], U32, name="e_codes", tag="e_codes", align_bytes=64)
+            e_scales = work.tile([P, 2 * P], U8, name="e_scales", tag="e_scales", align_bytes=64)
+            nc.vector.quantize_mx(
+                out=e_codes[:].bitcast(FP8X4),
+                scales=e_scales[:],
+                in_=live["e_grouped", g][:].rearrange("p i r t -> p (i r t)"),
+            )
+            live["e_codes", g] = e_codes
+            live["e_scales", g] = e_scales
+
+        def attend(g):
+            if not 0 <= g < PAIRS:
+                return
+            acc_ps = psum_mx.tile([P, 2, DIM], F32, name="acc_ps", tag="mx")
+            for i in range(2):
+                rows = slice(i * P, (i + 1) * P)
+                nc.tensor.matmul_mx(
+                    out=acc_ps[:, i, :],
+                    lhsT=live["e_codes", g][:, rows].bitcast(FP8X4),
+                    lhsT_scale=live["e_scales", g][:, rows],
+                    rhs=live["v_codes", g // 2][:].bitcast(FP8X4),
+                    rhs_scale=live["v_scales", g // 2][:],
+                    start=True,
+                    stop=True,
+                )
+            live["acc_ps", g] = acc_ps
+
+        def finish(g):
+            if not 0 <= g < PAIRS:
+                return
+            b, half = g // 2, g % 2
+            inv_sum = small.tile([P, 2], F32, name="inv_sum", tag="inv_sum")
+            nc.vector.reciprocal(out=inv_sum[:], in_=live["e_sum", g][:])
+            o_sb = work.tile([P, 2 * DIM], F32, name="o_sb", tag="o_sb", bufs=4)
+            for i in range(2):
+                first = (2 * half + i) * DIM
+                nc.vector.scalar_tensor_tensor(
+                    out=o_sb[:, i * DIM : (i + 1) * DIM],
+                    in0=live["acc_ps", g][:, i, :],
+                    scalar=inv_sum[:, i : i + 1],
+                    in1=live["x", b][:, first : first + DIM],
+                    op0=ALU.mult,
+                    op1=ALU.add,
+                )
+            out_rows = out[b].rearrange("(p i) c -> p (i c)", i=PACK)
+            nc.sync.dma_start(out=out_rows[:, 2 * half * DIM : 2 * (half + 1) * DIM], in_=o_sb[:])
+
+        for step in range(-3, PAIRS + 2):
+            odd = step % 2 == 1
+            transpose_e(step - 1)
+            transpose_y((step + 2) // 2, (step + 2) % 2)
+            quantise_e(step - 2)
+            if not odd:
+                quantise_y(step // 2)
+            exponentials(step)
+            attend(step - 2)
+            project_values(step // 2, step % 2)
+            scores(step + 2)
+            group_e(step - 1)
+            group_y((step + 2) // 2, (step + 2) % 2)
+            row_maxima(step + 1)
+            finish(step - 2)
+            if odd:
+                transpose_qk((step + 3) // 2)
+            group_v(step // 2, step % 2)
+            if odd:
+                quantise_v(step // 2)
+            else:
+                load_batch(step // 2 + 3)

@@ -10,7 +10,6 @@ U8 = mybir.dt.uint8
 FP8X4 = mybir.dt.float8_e4m3fn_x4
 ACT = mybir.ActivationFunctionType
 ALU = mybir.AluOpType
-AXIS = mybir.AxisListType
 
 BATCHES, ROWS, DIM, DY, HID = 16, 512, 256, 512, 128
 P = 128
@@ -26,40 +25,44 @@ def tile_block_pa_t_kernel(tc, q, k, y, Wv, x, out):
         const = ctx.enter_context(tc.tile_pool(name="const", bufs=1))
         loads = ctx.enter_context(tc.tile_pool(name="loads", bufs=4))
         work = ctx.enter_context(tc.tile_pool(name="work", bufs=3))
-        small = ctx.enter_context(tc.tile_pool(name="small", bufs=4))
-        psum_s = ctx.enter_context(tc.psum_pool(name="psum_s", bufs=4))
-        psum_tr = ctx.enter_context(tc.psum_pool(name="psum_tr", bufs=2))
-        psum_mx = ctx.enter_context(tc.psum_pool(name="psum_mx", bufs=2))
+        small = ctx.enter_context(tc.tile_pool(name="small", bufs=5))
+        psum = ctx.enter_context(tc.psum_pool(name="psum", bufs=8))
         ctx.enter_context(tc.manual_schedule())
 
         live = {}
 
-        def load_batch(b):
+        def load(name, src, b, bufs):
             if not 0 <= b < BATCHES:
                 return
-            for name, src, bufs in (("q", q, 4), ("k", k, 4), ("y", y, 4), ("x", x, 6)):
-                width = PACK * src.shape[2]
-                rows = loads.tile([P, width], BF16, name=name + "_sb", tag=name, bufs=bufs)
-                nc.sync.dma_start(out=rows[:], in_=src[b].rearrange("(p t) c -> p (t c)", t=PACK))
-                live[name, b] = rows
+            rows = loads.tile([P, PACK * src.shape[2]], BF16, name=name + "_sb", tag=name, bufs=bufs)
+            nc.sync.dma_start(out=rows[:], in_=src[b].rearrange("(p t) c -> p (t c)", t=PACK))
+            live[name, b] = rows
 
-        load_batch(0)
+        def load_qky(b):
+            load("q", q, b, 4)
+            load("k", k, b, 4)
+            load("y", y, b, 4)
+
+        load("q", q, 0, 4)
+        load("k", k, 0, 4)
         w_rows = const.tile([P, PACK, DIM], BF16, name="w_rows")
         for u in range(2):
             nc.sync.dma_start(
                 out=w_rows[:, 2 * u : 2 * u + 2, :],
                 in_=Wv[256 * u : 256 * (u + 1), :].rearrange("(p e) c -> p e c", e=2),
             )
-        load_batch(1)
-
-        warm = const.tile([P, 1], F32, name="warm")
-        nc.vector.memset(warm[:], 0.0)
-        nc.scalar.activation(out=warm[:], in_=warm[:], func=ACT.Exp)
+        load("y", y, 0, 4)
+        load_qky(1)
+        load_qky(2)
 
         ident_bf16 = const.tile([P, P], BF16, name="ident_bf16")
         make_identity(nc, ident_bf16[:])
         ident_f32 = const.tile([P, P], F32, name="ident_f32")
         make_identity(nc, ident_f32[:])
+
+        warm = const.tile([P, 1], F32, name="warm")
+        nc.vector.memset(warm[:], 0.0)
+        nc.scalar.activation(out=warm[:], in_=warm[:], func=ACT.Exp)
 
         w_grouped = const.tile([P, DIM, PACK], BF16, name="w_grouped", align_bytes=64)
         w_codes = const.tile([P, DIM], U32, name="w_codes", align_bytes=64)
@@ -74,7 +77,7 @@ def tile_block_pa_t_kernel(tc, q, k, y, Wv, x, out):
         def transpose_qk(b):
             if not 0 <= b < BATCHES:
                 return
-            qk_ps = psum_mx.tile([P, 2 * ROWS], BF16, name="qk_ps", tag="mx")
+            qk_ps = psum.tile([P, 2 * ROWS], BF16, name="qk_ps", tag="bank")
             for m, name in enumerate(("q", "k")):
                 for t in range(PACK):
                     nc.tensor.transpose(
@@ -82,15 +85,20 @@ def tile_block_pa_t_kernel(tc, q, k, y, Wv, x, out):
                         live[name, b][:, t * HID : (t + 1) * HID],
                         ident_bf16[:],
                     )
+            live["qk_ps", b] = qk_ps
+
+        def copy_qk(b):
+            if not 0 <= b < BATCHES:
+                return
             qk_t = work.tile([P, 2 * ROWS], BF16, name="qk_t", tag="qk_t")
-            nc.scalar.copy(out=qk_t[:], in_=qk_ps[:])
+            nc.scalar.copy(out=qk_t[:], in_=live["qk_ps", b][:])
             live["qk_t", b] = qk_t
 
         def transpose_y(b, half):
             if not 0 <= b < BATCHES:
                 return
             y_words = live["y", b][:].bitcast(F32)
-            yt_ps = psum_tr.tile([P, 2, 2, P], F32, name="yt_ps", tag="tr")
+            yt_ps = psum.tile([P, 2, 2, P], F32, name="yt_ps", tag="bank")
             for a in range(2):
                 for u in range(2):
                     first = (2 * half + a) * (DY // 2) + u * P
@@ -122,7 +130,7 @@ def tile_block_pa_t_kernel(tc, q, k, y, Wv, x, out):
         def project_values(b, half):
             if not 0 <= b < BATCHES:
                 return
-            v_ps = psum_mx.tile([P, PACK, P], F32, name="v_ps", tag="mx")
+            v_ps = psum.tile([P, PACK, P], F32, name="v_ps", tag="bank")
             cols = slice(half * P, (half + 1) * P)
             for t in range(PACK):
                 keys = slice(t * P, (t + 1) * P)
@@ -168,7 +176,7 @@ def tile_block_pa_t_kernel(tc, q, k, y, Wv, x, out):
             qk_t = live["qk_t", g // 2]
             for i in range(2):
                 tile_i = 2 * (g % 2) + i
-                s_ps = psum_s.tile([P, ROWS], F32, name="s_ps", tag="s")
+                s_ps = psum.tile([P, ROWS], F32, name="s_ps", tag="bank")
                 nc.tensor.matmul(
                     out=s_ps[:],
                     lhsT=qk_t[:, tile_i * P : (tile_i + 1) * P],
@@ -178,37 +186,46 @@ def tile_block_pa_t_kernel(tc, q, k, y, Wv, x, out):
                 )
                 live["s_ps", g, i] = s_ps
 
-        def row_maxima(g):
+        def scale_scores(g):
             if not 0 <= g < PAIRS:
                 return
-            top = small.tile([P, 2], F32, name="top", tag="top")
-            for i in range(2):
-                nc.vector.tensor_reduce(out=top[:, i : i + 1], in_=live["s_ps", g, i][:], axis=AXIS.X, op=ALU.max)
+            neg_s = work.tile([P, 2, ROWS], F32, name="neg_s", tag="neg_s")
             shift = small.tile([P, 2], F32, name="shift", tag="shift")
-            nc.gpsimd.tensor_scalar(out=shift[:], in0=top[:], scalar1=-SCALE, scalar2=0.0, op0=ALU.mult, op1=ALU.add)
+            for i in range(2):
+                nc.vector.tensor_scalar(
+                    out=neg_s[:, i, :],
+                    in0=live["s_ps", g, i][:],
+                    scalar1=-SCALE,
+                    scalar2=None,
+                    op0=ALU.mult,
+                    op1=ALU.min,
+                    accum_out=shift[:, i : i + 1],
+                )
+            live["neg_s", g] = neg_s
             live["shift", g] = shift
 
         def exponentials(g):
             if not 0 <= g < PAIRS:
                 return
+            b, half = divmod(g, 2)
+            if half == 0:
+                live["e_sum", b] = small.tile([P, PACK], F32, name="e_sum", tag="e_sum")
             e_sb = work.tile([P, 2, ROWS], BF16, name="e_sb", tag="e_sb")
-            e_sum = small.tile([P, 2], F32, name="e_sum", tag="e_sum")
             for i in range(2):
                 nc.scalar.activation(
                     out=e_sb[:, i, :],
-                    in_=live["s_ps", g, i][:],
+                    in_=live["neg_s", g][:, i, :],
                     func=ACT.Exp,
                     bias=live["shift", g][:, i : i + 1],
-                    scale=SCALE,
-                    accum_out=e_sum[:, i : i + 1],
+                    scale=-1.0,
+                    accum_out=live["e_sum", b][:, 2 * half + i : 2 * half + i + 1],
                 )
             live["e_sb", g] = e_sb
-            live["e_sum", g] = e_sum
 
         def transpose_e(g):
             if not 0 <= g < PAIRS:
                 return
-            et_ps = psum_tr.tile([P, 2, PACK, P], BF16, name="et_ps", tag="tr")
+            et_ps = psum.tile([P, 2, PACK, P], BF16, name="et_ps", tag="bank")
             for i in range(2):
                 for t in range(PACK):
                     nc.tensor.transpose(et_ps[:, i, t, :], live["e_sb", g][:, i, t * P : (t + 1) * P], ident_bf16[:])
@@ -237,7 +254,7 @@ def tile_block_pa_t_kernel(tc, q, k, y, Wv, x, out):
         def attend(g):
             if not 0 <= g < PAIRS:
                 return
-            acc_ps = psum_mx.tile([P, 2, DIM], F32, name="acc_ps", tag="mx")
+            acc_ps = psum.tile([P, 2, DIM], F32, name="acc_ps", tag="bank")
             for i in range(2):
                 rows = slice(i * P, (i + 1) * P)
                 nc.tensor.matmul_mx(
@@ -254,42 +271,46 @@ def tile_block_pa_t_kernel(tc, q, k, y, Wv, x, out):
         def finish(g):
             if not 0 <= g < PAIRS:
                 return
-            b, half = g // 2, g % 2
-            inv_sum = small.tile([P, 2], F32, name="inv_sum", tag="inv_sum")
-            nc.vector.reciprocal(out=inv_sum[:], in_=live["e_sum", g][:])
+            b, half = divmod(g, 2)
+            if half == 0:
+                inv_sum = small.tile([P, PACK], F32, name="inv_sum", tag="inv_sum")
+                nc.vector.reciprocal(out=inv_sum[:], in_=live["e_sum", b][:])
+                live["inv_sum", b] = inv_sum
             o_sb = work.tile([P, 2 * DIM], F32, name="o_sb", tag="o_sb", bufs=4)
             for i in range(2):
-                first = (2 * half + i) * DIM
+                tile_i = 2 * half + i
                 nc.vector.scalar_tensor_tensor(
                     out=o_sb[:, i * DIM : (i + 1) * DIM],
                     in0=live["acc_ps", g][:, i, :],
-                    scalar=inv_sum[:, i : i + 1],
-                    in1=live["x", b][:, first : first + DIM],
+                    scalar=live["inv_sum", b][:, tile_i : tile_i + 1],
+                    in1=live["x", b][:, tile_i * DIM : (tile_i + 1) * DIM],
                     op0=ALU.mult,
                     op1=ALU.add,
                 )
             out_rows = out[b].rearrange("(p i) c -> p (i c)", i=PACK)
             nc.sync.dma_start(out=out_rows[:, 2 * half * DIM : 2 * (half + 1) * DIM], in_=o_sb[:])
 
-        for step in range(-3, PAIRS + 2):
-            odd = step % 2 == 1
-            transpose_e(step - 1)
-            transpose_y((step + 2) // 2, (step + 2) % 2)
-            quantise_e(step - 2)
-            if not odd:
-                quantise_y(step // 2)
+        for step in range(-4, PAIRS + 5):
+            even = step % 2 == 0
+            group_e(step - 2)
+            if not even:
+                copy_qk((step + 3) // 2)
+            group_y(*divmod(step + 3, 2))
             exponentials(step)
-            attend(step - 2)
-            project_values(step // 2, step % 2)
+            scale_scores(step + 1)
+            quantise_e(step - 3)
+            if not even:
+                quantise_y((step + 1) // 2)
+                quantise_v((step - 3) // 2)
+            finish(step - 5)
+            group_v(*divmod(step - 1, 2))
             scores(step + 2)
-            group_e(step - 1)
-            group_y((step + 2) // 2, (step + 2) % 2)
-            row_maxima(step + 1)
-            finish(step - 2)
-            if odd:
-                transpose_qk((step + 3) // 2)
-            group_v(step // 2, step % 2)
-            if odd:
-                quantise_v(step // 2)
-            else:
-                load_batch(step // 2 + 3)
+            transpose_e(step - 1)
+            if even:
+                transpose_qk((step + 4) // 2)
+            transpose_y(*divmod(step + 4, 2))
+            attend(step - 4)
+            project_values(*divmod(step, 2))
+            if even:
+                load_qky((step + 4) // 2 + 3)
+                load("x", x, (step + 4) // 2, 6)

@@ -213,8 +213,8 @@ def tile_block_pa_t_kernel(tc, q, k, y, Wv, x, out):
             e_sb = work.tile([P, 2, ROWS], BF16, name="e_sb", tag="e_sb")
             for i in range(2):
                 nc.scalar.activation(
-                    out=e_sb[:, i, :],
-                    in_=live["neg_s", g][:, i, :],
+                    out=e_sb[:, i, :].rearrange("p (u m e) -> p u m e", u=2, e=2),
+                    in_=live["neg_s", g][:, i, :].rearrange("p (u e m) -> p u m e", u=2, e=2),
                     func=ACT.Exp,
                     bias=live["shift", g][:, i : i + 1],
                     scale=-1.0,
@@ -225,17 +225,20 @@ def tile_block_pa_t_kernel(tc, q, k, y, Wv, x, out):
         def transpose_e(g):
             if not 0 <= g < PAIRS:
                 return
-            et_ps = psum.tile([P, 2, PACK, P], BF16, name="et_ps", tag="bank")
+            e_words = live["e_sb", g][:].rearrange("p i c -> p (i c)").bitcast(F32)
+            et_ps = psum.tile([P, 2, 2, P], F32, name="et_ps", tag="bank")
             for i in range(2):
-                for t in range(PACK):
-                    nc.tensor.transpose(et_ps[:, i, t, :], live["e_sb", g][:, i, t * P : (t + 1) * P], ident_bf16[:])
+                for u in range(2):
+                    first = (2 * i + u) * P
+                    nc.tensor.transpose(et_ps[:, i, u, :], e_words[:, first : first + P], ident_f32[:])
             live["et_ps", g] = et_ps
 
         def group_e(g):
             if not 0 <= g < PAIRS:
                 return
             e_grouped = work.tile([P, 2, P, PACK], BF16, name="e_grouped", tag="e_grouped", align_bytes=64)
-            nc.scalar.copy(out=e_grouped[:], in_=live["et_ps", g][:].rearrange("p i t r -> p i r t"))
+            words = e_grouped[:].rearrange("p i r t -> p (i r t)").bitcast(F32).rearrange("p (i r u) -> p i r u", i=2, u=2)
+            nc.scalar.copy(out=words, in_=live["et_ps", g][:].rearrange("p i u r -> p i r u"))
             live["e_grouped", g] = e_grouped
 
         def quantise_e(g):

@@ -152,7 +152,8 @@ def tile_block_pa_t_kernel(tc, q, k, y, Wv, x, out):
                 live["v_grouped", b] = work.tile(
                     [P, DIM, PACK], BF16, name="v_grouped", tag="v_grouped", align_bytes=64
                 )
-            nc.vector.tensor_copy(
+            copy = nc.scalar.copy if half == 0 else nc.vector.tensor_copy
+            copy(
                 out=live["v_grouped", b][:, half * P : (half + 1) * P, :],
                 in_=live["v_ps", b, half][:].rearrange("p t c -> p c t"),
             )

@@ -272,14 +272,17 @@ def tile_block_pa_t_kernel(tc, q, k, y, Wv, x, out):
                 )
             live["acc_ps", g] = acc_ps
 
+        def invert_sums(b):
+            if not 0 <= b < BATCHES:
+                return
+            inv_sum = small.tile([P, PACK], F32, name="inv_sum", tag="inv_sum")
+            nc.vector.reciprocal(out=inv_sum[:], in_=live["e_sum", b][:])
+            live["inv_sum", b] = inv_sum
+
         def finish(g):
             if not 0 <= g < PAIRS:
                 return
             b, half = divmod(g, 2)
-            if half == 0:
-                inv_sum = small.tile([P, PACK], F32, name="inv_sum", tag="inv_sum")
-                nc.vector.reciprocal(out=inv_sum[:], in_=live["e_sum", b][:])
-                live["inv_sum", b] = inv_sum
             o_sb = work.tile([P, 2 * DIM], F32, name="o_sb", tag="o_sb", bufs=4)
             for i in range(2):
                 tile_i = 2 * half + i
@@ -308,6 +311,8 @@ def tile_block_pa_t_kernel(tc, q, k, y, Wv, x, out):
                 quantise_v((step - 3) // 2)
             finish(step - 5)
             group_v(*divmod(step - 1, 2))
+            if even:
+                invert_sums((step - 2) // 2)
             scores(step + 2)
             transpose_e(step - 1)
             if even:

@@ -24,7 +24,7 @@ def tile_block_pa_t_kernel(tc, q, k, y, Wv, x, out):
     with ExitStack() as ctx:
         const = ctx.enter_context(tc.tile_pool(name="const", bufs=1))
         loads = ctx.enter_context(tc.tile_pool(name="loads", bufs=4))
-        work = ctx.enter_context(tc.tile_pool(name="work", bufs=3))
+        work = ctx.enter_context(tc.tile_pool(name="work", bufs=5))
         small = ctx.enter_context(tc.tile_pool(name="small", bufs=5))
         psum = ctx.enter_context(tc.psum_pool(name="psum", bufs=8))
         ctx.enter_context(tc.manual_schedule())
@@ -283,7 +283,7 @@ def tile_block_pa_t_kernel(tc, q, k, y, Wv, x, out):
             if not 0 <= g < PAIRS:
                 return
             b, half = divmod(g, 2)
-            o_sb = work.tile([P, 2 * DIM], F32, name="o_sb", tag="o_sb", bufs=4)
+            o_sb = work.tile([P, 2 * DIM], F32, name="o_sb", tag="o_sb", bufs=PAIRS)
             for i in range(2):
                 tile_i = 2 * half + i
                 nc.vector.scalar_tensor_tensor(
@@ -322,4 +322,4 @@ def tile_block_pa_t_kernel(tc, q, k, y, Wv, x, out):
             project_values(*divmod(step, 2))
             if even:
                 load_qky((step + 4) // 2 + 3)
-                load("x", x, (step + 4) // 2, 6)
+                load("x", x, (step + 4) // 2, BATCHES)

@@ -45,13 +45,18 @@ def tile_block_pa_t_kernel(tc, q, k, y, Wv, x, out):
 
         load("q", q, 0, 4)
         load("k", k, 0, 4)
+        y_rows = loads.tile([P, PACK * DY], BF16, name="y_sb", tag="y", bufs=4)
+        y_src = y[0].rearrange("(p t) c -> p (t c)", t=PACK)
+        for half in range(2):
+            cols = slice(2 * half * DY, 2 * (half + 1) * DY)
+            nc.sync.dma_start(out=y_rows[:, cols], in_=y_src[:, cols])
+        live["y", 0] = y_rows
         w_rows = const.tile([P, PACK, DIM], BF16, name="w_rows")
         for u in range(2):
             nc.sync.dma_start(
                 out=w_rows[:, 2 * u : 2 * u + 2, :],
                 in_=Wv[256 * u : 256 * (u + 1), :].rearrange("(p e) c -> p e c", e=2),
             )
-        load("y", y, 0, 4)
         load_qky(1)
         load_qky(2)
 
@@ -67,15 +72,17 @@ def tile_block_pa_t_kernel(tc, q, k, y, Wv, x, out):
         w_grouped = const.tile([P, DIM, PACK], BF16, name="w_grouped", align_bytes=64)
         w_codes = const.tile([P, DIM], U32, name="w_codes", align_bytes=64)
         w_scales = const.tile([P, DIM], U8, name="w_scales", align_bytes=64)
-        nc.vector.tensor_copy(out=w_grouped[:], in_=w_rows[:].rearrange("p t c -> p c t"))
-        nc.vector.quantize_mx(
-            out=w_codes[:].bitcast(FP8X4),
-            scales=w_scales[:],
-            in_=w_grouped[:].rearrange("p c t -> p (c t)"),
+        nc.gpsimd.tensor_scalar(
+            out=w_grouped[:],
+            in0=w_rows[:].rearrange("p t c -> p c t"),
+            scalar1=1.0,
+            scalar2=0.0,
+            op0=ALU.mult,
+            op1=ALU.add,
         )
 
         def transpose_qk(b):
-            if not 0 <= b < BATCHES:
+            if not 0 <= b < BATCHES or ("qk_ps", b) in live:
                 return
             qk_ps = psum.tile([P, 2 * ROWS], BF16, name="qk_ps", tag="bank")
             for m, name in enumerate(("q", "k")):
@@ -88,14 +95,14 @@ def tile_block_pa_t_kernel(tc, q, k, y, Wv, x, out):
             live["qk_ps", b] = qk_ps
 
         def copy_qk(b):
-            if not 0 <= b < BATCHES:
+            if not 0 <= b < BATCHES or ("qk_t", b) in live:
                 return
             qk_t = work.tile([P, 2 * ROWS], BF16, name="qk_t", tag="qk_t")
             nc.scalar.copy(out=qk_t[:], in_=live["qk_ps", b][:])
             live["qk_t", b] = qk_t
 
         def transpose_y(b, half):
-            if not 0 <= b < BATCHES:
+            if not 0 <= b < BATCHES or ("yt_ps", b, half) in live:
                 return
             y_words = live["y", b][:].bitcast(F32)
             yt_ps = psum.tile([P, 2, 2, P], F32, name="yt_ps", tag="bank")
@@ -106,14 +113,16 @@ def tile_block_pa_t_kernel(tc, q, k, y, Wv, x, out):
             live["yt_ps", b, half] = yt_ps
 
         def group_y(b, half):
-            if not 0 <= b < BATCHES:
+            if not 0 <= b < BATCHES or ("words", b, half) in live:
                 return
             if half == 0:
                 live["y_grouped", b] = work.tile(
                     [P, ROWS * PACK], BF16, name="y_grouped", tag="y_grouped", align_bytes=64
                 )
             words = live["y_grouped", b][:].bitcast(F32).rearrange("p (a m u) -> p a m u", a=PACK, u=2)
-            nc.scalar.copy(
+            live["words", b, half] = words
+            copy = nc.scalar.copy
+            copy(
                 out=words[:, 2 * half : 2 * half + 2, :, :],
                 in_=live["yt_ps", b, half][:].rearrange("p a u m -> p a m u"),
             )
@@ -152,7 +161,7 @@ def tile_block_pa_t_kernel(tc, q, k, y, Wv, x, out):
                 live["v_grouped", b] = work.tile(
                     [P, DIM, PACK], BF16, name="v_grouped", tag="v_grouped", align_bytes=64
                 )
-            copy = nc.scalar.copy if half == 0 else nc.vector.tensor_copy
+            copy = nc.scalar.copy if (half == 0 and b >= 1) or b >= 15 else nc.vector.tensor_copy
             copy(
                 out=live["v_grouped", b][:, half * P : (half + 1) * P, :],
                 in_=live["v_ps", b, half][:].rearrange("p t c -> p c t"),
@@ -172,7 +181,7 @@ def tile_block_pa_t_kernel(tc, q, k, y, Wv, x, out):
             live["v_scales", b] = v_scales
 
         def scores(g):
-            if not 0 <= g < PAIRS:
+            if not 0 <= g < PAIRS or ("s_ps", g, 0) in live:
                 return
             qk_t = live["qk_t", g // 2]
             for i in range(2):
@@ -188,7 +197,7 @@ def tile_block_pa_t_kernel(tc, q, k, y, Wv, x, out):
                 live["s_ps", g, i] = s_ps
 
         def scale_scores(g):
-            if not 0 <= g < PAIRS:
+            if not 0 <= g < PAIRS or ("neg_s", g) in live:
                 return
             neg_s = work.tile([P, 2, ROWS], F32, name="neg_s", tag="neg_s")
             shift = small.tile([P, 2], F32, name="shift", tag="shift")
@@ -206,7 +215,7 @@ def tile_block_pa_t_kernel(tc, q, k, y, Wv, x, out):
             live["shift", g] = shift
 
         def exponentials(g):
-            if not 0 <= g < PAIRS:
+            if not 0 <= g < PAIRS or ("e_sb", g) in live:
                 return
             b, half = divmod(g, 2)
             if half == 0:
@@ -223,54 +232,65 @@ def tile_block_pa_t_kernel(tc, q, k, y, Wv, x, out):
                 )
             live["e_sb", g] = e_sb
 
+        def parts(g):
+            return ((0, 1), (1, 2)) if g == PAIRS - 1 else ((0, 2),)
+
         def transpose_e(g):
             if not 0 <= g < PAIRS:
                 return
             e_words = live["e_sb", g][:].rearrange("p i c -> p (i c)").bitcast(F32)
-            et_ps = psum.tile([P, 2, 2, P], F32, name="et_ps", tag="bank")
-            for i in range(2):
-                for u in range(2):
-                    first = (2 * i + u) * P
-                    nc.tensor.transpose(et_ps[:, i, u, :], e_words[:, first : first + P], ident_f32[:])
-            live["et_ps", g] = et_ps
+            for lo, hi in parts(g):
+                et_ps = psum.tile([P, hi - lo, 2, P], F32, name="et_ps", tag="bank")
+                for i in range(lo, hi):
+                    for u in range(2):
+                        first = (2 * i + u) * P
+                        nc.tensor.transpose(et_ps[:, i - lo, u, :], e_words[:, first : first + P], ident_f32[:])
+                live["et_ps", g, lo] = et_ps
 
         def group_e(g):
             if not 0 <= g < PAIRS:
                 return
-            e_grouped = work.tile([P, 2, P, PACK], BF16, name="e_grouped", tag="e_grouped", align_bytes=64)
-            words = e_grouped[:].rearrange("p i r t -> p (i r t)").bitcast(F32).rearrange("p (i r u) -> p i r u", i=2, u=2)
-            nc.scalar.copy(out=words, in_=live["et_ps", g][:].rearrange("p i u r -> p i r u"))
-            live["e_grouped", g] = e_grouped
+            for lo, hi in parts(g):
+                e_grouped = work.tile([P, hi - lo, P, PACK], BF16, name="e_grouped", tag="e_grouped", align_bytes=64)
+                words = e_grouped[:].rearrange("p i r t -> p (i r t)").bitcast(F32)
+                nc.scalar.copy(
+                    out=words.rearrange("p (i r u) -> p i r u", i=hi - lo, u=2),
+                    in_=live["et_ps", g, lo][:].rearrange("p i u r -> p i r u"),
+                )
+                live["e_grouped", g, lo] = e_grouped
 
         def quantise_e(g):
             if not 0 <= g < PAIRS:
                 return
-            e_codes = work.tile([P, 2 * P], U32, name="e_codes", tag="e_codes", align_bytes=64)
-            e_scales = work.tile([P, 2 * P], U8, name="e_scales", tag="e_scales", align_bytes=64)
-            nc.vector.quantize_mx(
-                out=e_codes[:].bitcast(FP8X4),
-                scales=e_scales[:],
-                in_=live["e_grouped", g][:].rearrange("p i r t -> p (i r t)"),
-            )
-            live["e_codes", g] = e_codes
-            live["e_scales", g] = e_scales
+            for lo, hi in parts(g):
+                n = (hi - lo) * P
+                e_codes = work.tile([P, n], U32, name="e_codes", tag="e_codes", align_bytes=64)
+                e_scales = work.tile([P, n], U8, name="e_scales", tag="e_scales", align_bytes=64)
+                nc.vector.quantize_mx(
+                    out=e_codes[:].bitcast(FP8X4),
+                    scales=e_scales[:],
+                    in_=live["e_grouped", g, lo][:].rearrange("p i r t -> p (i r t)"),
+                )
+                live["e_codes", g, lo] = e_codes
+                live["e_scales", g, lo] = e_scales
 
         def attend(g):
             if not 0 <= g < PAIRS:
                 return
-            acc_ps = psum.tile([P, 2, DIM], F32, name="acc_ps", tag="bank")
-            for i in range(2):
-                rows = slice(i * P, (i + 1) * P)
-                nc.tensor.matmul_mx(
-                    out=acc_ps[:, i, :],
-                    lhsT=live["e_codes", g][:, rows].bitcast(FP8X4),
-                    lhsT_scale=live["e_scales", g][:, rows],
-                    rhs=live["v_codes", g // 2][:].bitcast(FP8X4),
-                    rhs_scale=live["v_scales", g // 2][:],
-                    start=True,
-                    stop=True,
-                )
-            live["acc_ps", g] = acc_ps
+            for lo, hi in parts(g):
+                acc_ps = psum.tile([P, hi - lo, DIM], F32, name="acc_ps", tag="bank")
+                for i in range(hi - lo):
+                    rows = slice(i * P, (i + 1) * P)
+                    nc.tensor.matmul_mx(
+                        out=acc_ps[:, i, :],
+                        lhsT=live["e_codes", g, lo][:, rows].bitcast(FP8X4),
+                        lhsT_scale=live["e_scales", g, lo][:, rows],
+                        rhs=live["v_codes", g // 2][:].bitcast(FP8X4),
+                        rhs_scale=live["v_scales", g // 2][:],
+                        start=True,
+                        stop=True,
+                    )
+                live["acc_ps", g, lo] = acc_ps
 
         def invert_sums(b):
             if not 0 <= b < BATCHES:
@@ -284,19 +304,39 @@ def tile_block_pa_t_kernel(tc, q, k, y, Wv, x, out):
                 return
             b, half = divmod(g, 2)
             o_sb = work.tile([P, 2 * DIM], F32, name="o_sb", tag="o_sb", bufs=PAIRS)
-            for i in range(2):
-                tile_i = 2 * half + i
-                nc.vector.scalar_tensor_tensor(
-                    out=o_sb[:, i * DIM : (i + 1) * DIM],
-                    in0=live["acc_ps", g][:, i, :],
-                    scalar=live["inv_sum", b][:, tile_i : tile_i + 1],
-                    in1=live["x", b][:, tile_i * DIM : (tile_i + 1) * DIM],
-                    op0=ALU.mult,
-                    op1=ALU.add,
-                )
             out_rows = out[b].rearrange("(p i) c -> p (i c)", i=PACK)
-            nc.sync.dma_start(out=out_rows[:, 2 * half * DIM : 2 * (half + 1) * DIM], in_=o_sb[:])
+            for lo, hi in parts(g):
+                for i in range(lo, hi):
+                    tile_i = 2 * half + i
+                    nc.vector.scalar_tensor_tensor(
+                        out=o_sb[:, i * DIM : (i + 1) * DIM],
+                        in0=live["acc_ps", g, lo][:, i - lo, :],
+                        scalar=live["inv_sum", b][:, tile_i : tile_i + 1],
+                        in1=live["x", b][:, tile_i * DIM : (tile_i + 1) * DIM],
+                        op0=ALU.mult,
+                        op1=ALU.add,
+                    )
+                nc.sync.dma_start(
+                    out=out_rows[:, (2 * half + lo) * DIM : (2 * half + hi) * DIM],
+                    in_=o_sb[:, lo * DIM : hi * DIM],
+                )
 
+        transpose_qk(0)
+        copy_qk(0)
+        transpose_y(0, 0)
+        transpose_y(0, 1)
+        group_y(0, 0)
+        scores(0)
+        group_y(0, 1)
+        scale_scores(0)
+        transpose_qk(1)
+        copy_qk(1)
+        exponentials(0)
+        nc.vector.quantize_mx(
+            out=w_codes[:].bitcast(FP8X4),
+            scales=w_scales[:],
+            in_=w_grouped[:].rearrange("p c t -> p (c t)"),
+        )
         for step in range(-4, PAIRS + 5):
             even = step % 2 == 0
             group_e(step - 2)

@@ -349,17 +349,22 @@ def tile_block_pa_t_kernel(tc, q, k, y, Wv, x, out):
             if not even:
                 quantise_y((step + 1) // 2)
                 quantise_v((step - 3) // 2)
-            finish(step - 5)
-            group_v(*divmod(step - 1, 2))
             if even:
+                finish(step - 6)
+                finish(step - 5)
+                group_v((step - 2) // 2, 0)
+                group_v((step - 2) // 2, 1)
                 invert_sums((step - 2) // 2)
             scores(step + 2)
             transpose_e(step - 1)
             if even:
                 transpose_qk((step + 4) // 2)
             transpose_y(*divmod(step + 4, 2))
-            attend(step - 4)
-            project_values(*divmod(step, 2))
+            if not even:
+                attend(step - 5)
+                attend(step - 4)
+                project_values((step - 1) // 2, 0)
+                project_values((step - 1) // 2, 1)
             if even:
                 load_qky((step + 4) // 2 + 3)
                 load("x", x, (step + 4) // 2, BATCHES)

@@ -69,6 +69,16 @@ def tile_block_pa_t_kernel(tc, q, k, y, Wv, x, out):
         nc.vector.memset(warm[:], 0.0)
         nc.scalar.activation(out=warm[:], in_=warm[:], func=ACT.Exp)
 
+        zeros = const.tile([P, ROWS], BF16, name="zeros")
+        nc.vector.memset(zeros[:], 0.0)
+
+        def keep_warm(count):
+            idle_ps = psum.tile([P, ROWS], F32, name="idle_ps", tag="bank")
+            for repeat in range(count):
+                nc.tensor.matmul(out=idle_ps[:], lhsT=zeros[:, :P], rhs=zeros[:], start=True, stop=True)
+
+        keep_warm(4)
+
         w_grouped = const.tile([P, DIM, PACK], BF16, name="w_grouped", align_bytes=64)
         w_codes = const.tile([P, DIM], U32, name="w_codes", align_bytes=64)
         w_scales = const.tile([P, DIM], U8, name="w_scales", align_bytes=64)
@@ -357,6 +367,8 @@ def tile_block_pa_t_kernel(tc, q, k, y, Wv, x, out):
                 invert_sums((step - 2) // 2)
             scores(step + 2)
             transpose_e(step - 1)
+            if step in (PAIRS + 2, PAIRS + 3):
+                keep_warm(3)
             if even:
                 transpose_qk((step + 4) // 2)
             transpose_y(*divmod(step + 4, 2))

@@ -65,19 +65,19 @@ def tile_block_pa_t_kernel(tc, q, k, y, Wv, x, out):
         ident_f32 = const.tile([P, P], F32, name="ident_f32")
         make_identity(nc, ident_f32[:])
 
+        zeros = const.tile([P, P], BF16, name="zeros")
+        nc.vector.memset(zeros[:], 0.0)
         warm = const.tile([P, 1], F32, name="warm")
         nc.vector.memset(warm[:], 0.0)
         nc.scalar.activation(out=warm[:], in_=warm[:], func=ACT.Exp)
 
-        zeros = const.tile([P, ROWS], BF16, name="zeros")
-        nc.vector.memset(zeros[:], 0.0)
 
         def keep_warm(count):
-            idle_ps = psum.tile([P, ROWS], F32, name="idle_ps", tag="bank")
+            idle_ps = psum.tile([P, P], F32, name="idle_ps", tag="bank")
             for repeat in range(count):
-                nc.tensor.matmul(out=idle_ps[:], lhsT=zeros[:, :P], rhs=zeros[:], start=True, stop=True)
+                nc.tensor.matmul(out=idle_ps[:], lhsT=zeros[:], rhs=zeros[:], start=True, stop=True)
 
-        keep_warm(4)
+        keep_warm(12)
 
         w_grouped = const.tile([P, DIM, PACK], BF16, name="w_grouped", align_bytes=64)
         w_codes = const.tile([P, DIM], U32, name="w_codes", align_bytes=64)
@@ -171,7 +171,7 @@ def tile_block_pa_t_kernel(tc, q, k, y, Wv, x, out):
                 live["v_grouped", b] = work.tile(
                     [P, DIM, PACK], BF16, name="v_grouped", tag="v_grouped", align_bytes=64
                 )
-            copy = nc.scalar.copy if (half == 0 and b >= 1) or b >= 15 else nc.vector.tensor_copy
+            copy = nc.scalar.copy if (half == 0 and b >= 1) or b % 8 == 7 else nc.vector.tensor_copy
             copy(
                 out=live["v_grouped", b][:, half * P : (half + 1) * P, :],
                 in_=live["v_ps", b, half][:].rearrange("p t c -> p c t"),
@@ -368,7 +368,7 @@ def tile_block_pa_t_kernel(tc, q, k, y, Wv, x, out):
             scores(step + 2)
             transpose_e(step - 1)
             if step in (PAIRS + 2, PAIRS + 3):
-                keep_warm(3)
+                keep_warm(12)
             if even:
                 transpose_qk((step + 4) // 2)
             transpose_y(*divmod(step + 4, 2))

from contextlib import ExitStack

import concourse.mybir as mybir
from concourse.masks import make_identity

F32 = mybir.dt.float32
BF16 = mybir.dt.bfloat16
U32 = mybir.dt.uint32
U8 = mybir.dt.uint8
FP8X4 = mybir.dt.float8_e4m3fn_x4
ACT = mybir.ActivationFunctionType
ALU = mybir.AluOpType

BATCHES, ROWS, DIM, DY, HID = 16, 512, 256, 512, 128
P = 128
PACK = 4
PAIRS = 2 * BATCHES
SCALE = HID ** -0.5
FLOPS = 2 * BATCHES * ROWS * (DY * DIM + ROWS * HID + ROWS * DIM)


def tile_block_pa_t_kernel(tc, q, k, y, Wv, x, out):
    nc = tc.nc
    with ExitStack() as ctx:
        const = ctx.enter_context(tc.tile_pool(name="const", bufs=1))
        loads = ctx.enter_context(tc.tile_pool(name="loads", bufs=4))
        work = ctx.enter_context(tc.tile_pool(name="work", bufs=5))
        small = ctx.enter_context(tc.tile_pool(name="small", bufs=5))
        psum = ctx.enter_context(tc.psum_pool(name="psum", bufs=8))
        ctx.enter_context(tc.manual_schedule())

        live = {}

        def load(name, src, b, bufs):
            if not 0 <= b < BATCHES:
                return
            rows = loads.tile([P, PACK * src.shape[2]], BF16, name=name + "_sb", tag=name, bufs=bufs)
            nc.sync.dma_start(out=rows[:], in_=src[b].rearrange("(p t) c -> p (t c)", t=PACK))
            live[name, b] = rows

        def load_qky(b):
            load("q", q, b, 4)
            load("k", k, b, 4)
            load("y", y, b, 4)

        load("q", q, 0, 4)
        load("k", k, 0, 4)
        y_rows = loads.tile([P, PACK * DY], BF16, name="y_sb", tag="y", bufs=4)
        y_src = y[0].rearrange("(p t) c -> p (t c)", t=PACK)
        for half in range(2):
            cols = slice(2 * half * DY, 2 * (half + 1) * DY)
            nc.sync.dma_start(out=y_rows[:, cols], in_=y_src[:, cols])
        live["y", 0] = y_rows
        w_rows = const.tile([P, PACK, DIM], BF16, name="w_rows")
        for u in range(2):
            nc.sync.dma_start(
                out=w_rows[:, 2 * u : 2 * u + 2, :],
                in_=Wv[256 * u : 256 * (u + 1), :].rearrange("(p e) c -> p e c", e=2),
            )
        load_qky(1)
        load_qky(2)

        ident_bf16 = const.tile([P, P], BF16, name="ident_bf16")
        make_identity(nc, ident_bf16[:])
        ident_f32 = const.tile([P, P], F32, name="ident_f32")
        make_identity(nc, ident_f32[:])

        zeros = const.tile([P, P], BF16, name="zeros")
        nc.vector.memset(zeros[:], 0.0)
        warm = const.tile([P, 1], F32, name="warm")
        nc.vector.memset(warm[:], 0.0)
        nc.scalar.activation(out=warm[:], in_=warm[:], func=ACT.Exp)


        def keep_warm(count):
            idle_ps = psum.tile([P, P], F32, name="idle_ps", tag="bank")
            for repeat in range(count):
                nc.tensor.matmul(out=idle_ps[:], lhsT=zeros[:], rhs=zeros[:], start=True, stop=True)

        keep_warm(12)

        w_grouped = const.tile([P, DIM, PACK], BF16, name="w_grouped", align_bytes=64)
        w_codes = const.tile([P, DIM], U32, name="w_codes", align_bytes=64)
        w_scales = const.tile([P, DIM], U8, name="w_scales", align_bytes=64)
        nc.gpsimd.tensor_scalar(
            out=w_grouped[:],
            in0=w_rows[:].rearrange("p t c -> p c t"),
            scalar1=1.0,
            scalar2=0.0,
            op0=ALU.mult,
            op1=ALU.add,
        )

        def transpose_qk(b):
            if not 0 <= b < BATCHES or ("qk_ps", b) in live:
                return
            qk_ps = psum.tile([P, 2 * ROWS], BF16, name="qk_ps", tag="bank")
            for m, name in enumerate(("q", "k")):
                for t in range(PACK):
                    nc.tensor.transpose(
                        qk_ps[:, m * ROWS + t * P : m * ROWS + (t + 1) * P],
                        live[name, b][:, t * HID : (t + 1) * HID],
                        ident_bf16[:],
                    )
            live["qk_ps", b] = qk_ps

        def copy_qk(b):
            if not 0 <= b < BATCHES or ("qk_t", b) in live:
                return
            qk_t = work.tile([P, 2 * ROWS], BF16, name="qk_t", tag="qk_t")
            nc.scalar.copy(out=qk_t[:], in_=live["qk_ps", b][:])
            live["qk_t", b] = qk_t

        def transpose_y(b, half):
            if not 0 <= b < BATCHES or ("yt_ps", b, half) in live:
                return
            y_words = live["y", b][:].bitcast(F32)
            yt_ps = psum.tile([P, 2, 2, P], F32, name="yt_ps", tag="bank")
            for a in range(2):
                for u in range(2):
                    first = (2 * half + a) * (DY // 2) + u * P
                    nc.tensor.transpose(yt_ps[:, a, u, :], y_words[:, first : first + P], ident_f32[:])
            live["yt_ps", b, half] = yt_ps

        def group_y(b, half):
            if not 0 <= b < BATCHES or ("words", b, half) in live:
                return
            if half == 0:
                live["y_grouped", b] = work.tile(
                    [P, ROWS * PACK], BF16, name="y_grouped", tag="y_grouped", align_bytes=64
                )
            words = live["y_grouped", b][:].bitcast(F32).rearrange("p (a m u) -> p a m u", a=PACK, u=2)
            live["words", b, half] = words
            copy = nc.scalar.copy
            copy(
                out=words[:, 2 * half : 2 * half + 2, :, :],
                in_=live["yt_ps", b, half][:].rearrange("p a u m -> p a m u"),
            )

        def quantise_y(b):
            if not 0 <= b < BATCHES:
                return
            y_codes = work.tile([P, ROWS], U32, name="y_codes", tag="y_codes", align_bytes=64)
            y_scales = work.tile([P, ROWS], U8, name="y_scales", tag="y_scales", align_bytes=64)
            nc.vector.quantize_mx(out=y_codes[:].bitcast(FP8X4), scales=y_scales[:], in_=live["y_grouped", b][:])
            live["y_codes", b] = y_codes
            live["y_scales", b] = y_scales

        def project_values(b, half):
            if not 0 <= b < BATCHES:
                return
            v_ps = psum.tile([P, PACK, P], F32, name="v_ps", tag="bank")
            cols = slice(half * P, (half + 1) * P)
            for t in range(PACK):
                keys = slice(t * P, (t + 1) * P)
                nc.tensor.matmul_mx(
                    out=v_ps[:, t, :],
                    lhsT=live["y_codes", b][:, keys].bitcast(FP8X4),
                    lhsT_scale=live["y_scales", b][:, keys],
                    rhs=w_codes[:, cols].bitcast(FP8X4),
                    rhs_scale=w_scales[:, cols],
                    start=True,
                    stop=True,
                )
            live["v_ps", b, half] = v_ps

        def group_v(b, half):
            if not 0 <= b < BATCHES:
                return
            if half == 0:
                live["v_grouped", b] = work.tile(
                    [P, DIM, PACK], BF16, name="v_grouped", tag="v_grouped", align_bytes=64
                )
            copy = nc.scalar.copy if (half == 0 and b >= 1) or b % 8 == 7 else nc.vector.tensor_copy
            copy(
                out=live["v_grouped", b][:, half * P : (half + 1) * P, :],
                in_=live["v_ps", b, half][:].rearrange("p t c -> p c t"),
            )

        def quantise_v(b):
            if not 0 <= b < BATCHES:
                return
            v_codes = work.tile([P, DIM], U32, name="v_codes", tag="v_codes", align_bytes=64)
            v_scales = work.tile([P, DIM], U8, name="v_scales", tag="v_scales", align_bytes=64)
            nc.vector.quantize_mx(
                out=v_codes[:].bitcast(FP8X4),
                scales=v_scales[:],
                in_=live["v_grouped", b][:].rearrange("p c t -> p (c t)"),
            )
            live["v_codes", b] = v_codes
            live["v_scales", b] = v_scales

        def scores(g):
            if not 0 <= g < PAIRS or ("s_ps", g, 0) in live:
                return
            qk_t = live["qk_t", g // 2]
            for i in range(2):
                tile_i = 2 * (g % 2) + i
                s_ps = psum.tile([P, ROWS], F32, name="s_ps", tag="bank")
                nc.tensor.matmul(
                    out=s_ps[:],
                    lhsT=qk_t[:, tile_i * P : (tile_i + 1) * P],
                    rhs=qk_t[:, ROWS : 2 * ROWS],
                    start=True,
                    stop=True,
                )
                live["s_ps", g, i] = s_ps

        def scale_scores(g):
            if not 0 <= g < PAIRS or ("neg_s", g) in live:
                return
            neg_s = work.tile([P, 2, ROWS], F32, name="neg_s", tag="neg_s")
            shift = small.tile([P, 2], F32, name="shift", tag="shift")
            for i in range(2):
                nc.vector.tensor_scalar(
                    out=neg_s[:, i, :],
                    in0=live["s_ps", g, i][:],
                    scalar1=-SCALE,
                    scalar2=None,
                    op0=ALU.mult,
                    op1=ALU.min,
                    accum_out=shift[:, i : i + 1],
                )
            live["neg_s", g] = neg_s
            live["shift", g] = shift

        def exponentials(g):
            if not 0 <= g < PAIRS or ("e_sb", g) in live:
                return
            b, half = divmod(g, 2)
            if half == 0:
                live["e_sum", b] = small.tile([P, PACK], F32, name="e_sum", tag="e_sum")
            e_sb = work.tile([P, 2, ROWS], BF16, name="e_sb", tag="e_sb")
            for i in range(2):
                nc.scalar.activation(
                    out=e_sb[:, i, :].rearrange("p (u m e) -> p u m e", u=2, e=2),
                    in_=live["neg_s", g][:, i, :].rearrange("p (u e m) -> p u m e", u=2, e=2),
                    func=ACT.Exp,
                    bias=live["shift", g][:, i : i + 1],
                    scale=-1.0,
                    accum_out=live["e_sum", b][:, 2 * half + i : 2 * half + i + 1],
                )
            live["e_sb", g] = e_sb

        def parts(g):
            return ((0, 1), (1, 2)) if g == PAIRS - 1 else ((0, 2),)

        def transpose_e(g):
            if not 0 <= g < PAIRS:
                return
            e_words = live["e_sb", g][:].rearrange("p i c -> p (i c)").bitcast(F32)
            for lo, hi in parts(g):
                et_ps = psum.tile([P, hi - lo, 2, P], F32, name="et_ps", tag="bank")
                for i in range(lo, hi):
                    for u in range(2):
                        first = (2 * i + u) * P
                        nc.tensor.transpose(et_ps[:, i - lo, u, :], e_words[:, first : first + P], ident_f32[:])
                live["et_ps", g, lo] = et_ps

        def group_e(g):
            if not 0 <= g < PAIRS:
                return
            for lo, hi in parts(g):
                e_grouped = work.tile([P, hi - lo, P, PACK], BF16, name="e_grouped", tag="e_grouped", align_bytes=64)
                words = e_grouped[:].rearrange("p i r t -> p (i r t)").bitcast(F32)
                nc.scalar.copy(
                    out=words.rearrange("p (i r u) -> p i r u", i=hi - lo, u=2),
                    in_=live["et_ps", g, lo][:].rearrange("p i u r -> p i r u"),
                )
                live["e_grouped", g, lo] = e_grouped

        def quantise_e(g):
            if not 0 <= g < PAIRS:
                return
            for lo, hi in parts(g):
                n = (hi - lo) * P
                e_codes = work.tile([P, n], U32, name="e_codes", tag="e_codes", align_bytes=64)
                e_scales = work.tile([P, n], U8, name="e_scales", tag="e_scales", align_bytes=64)
                nc.vector.quantize_mx(
                    out=e_codes[:].bitcast(FP8X4),
                    scales=e_scales[:],
                    in_=live["e_grouped", g, lo][:].rearrange("p i r t -> p (i r t)"),
                )
                live["e_codes", g, lo] = e_codes
                live["e_scales", g, lo] = e_scales

        def attend(g):
            if not 0 <= g < PAIRS:
                return
            for lo, hi in parts(g):
                acc_ps = psum.tile([P, hi - lo, DIM], F32, name="acc_ps", tag="bank")
                for i in range(hi - lo):
                    rows = slice(i * P, (i + 1) * P)
                    nc.tensor.matmul_mx(
                        out=acc_ps[:, i, :],
                        lhsT=live["e_codes", g, lo][:, rows].bitcast(FP8X4),
                        lhsT_scale=live["e_scales", g, lo][:, rows],
                        rhs=live["v_codes", g // 2][:].bitcast(FP8X4),
                        rhs_scale=live["v_scales", g // 2][:],
                        start=True,
                        stop=True,
                    )
                live["acc_ps", g, lo] = acc_ps

        def invert_sums(b):
            if not 0 <= b < BATCHES:
                return
            inv_sum = small.tile([P, PACK], F32, name="inv_sum", tag="inv_sum")
            nc.vector.reciprocal(out=inv_sum[:], in_=live["e_sum", b][:])
            live["inv_sum", b] = inv_sum

        def finish(g):
            if not 0 <= g < PAIRS:
                return
            b, half = divmod(g, 2)
            o_sb = work.tile([P, 2 * DIM], F32, name="o_sb", tag="o_sb", bufs=PAIRS)
            out_rows = out[b].rearrange("(p i) c -> p (i c)", i=PACK)
            for lo, hi in parts(g):
                for i in range(lo, hi):
                    tile_i = 2 * half + i
                    nc.vector.scalar_tensor_tensor(
                        out=o_sb[:, i * DIM : (i + 1) * DIM],
                        in0=live["acc_ps", g, lo][:, i - lo, :],
                        scalar=live["inv_sum", b][:, tile_i : tile_i + 1],
                        in1=live["x", b][:, tile_i * DIM : (tile_i + 1) * DIM],
                        op0=ALU.mult,
                        op1=ALU.add,
                    )
                nc.sync.dma_start(
                    out=out_rows[:, (2 * half + lo) * DIM : (2 * half + hi) * DIM],
                    in_=o_sb[:, lo * DIM : hi * DIM],
                )

        transpose_qk(0)
        copy_qk(0)
        transpose_y(0, 0)
        transpose_y(0, 1)
        group_y(0, 0)
        scores(0)
        group_y(0, 1)
        scale_scores(0)
        transpose_qk(1)
        copy_qk(1)
        exponentials(0)
        nc.vector.quantize_mx(
            out=w_codes[:].bitcast(FP8X4),
            scales=w_scales[:],
            in_=w_grouped[:].rearrange("p c t -> p (c t)"),
        )
        for step in range(-4, PAIRS + 5):
            even = step % 2 == 0
            group_e(step - 2)
            if not even:
                copy_qk((step + 3) // 2)
            group_y(*divmod(step + 3, 2))
            exponentials(step)
            scale_scores(step + 1)
            quantise_e(step - 3)
            if not even:
                quantise_y((step + 1) // 2)
                quantise_v((step - 3) // 2)
            if even:
                finish(step - 6)
                finish(step - 5)
                group_v((step - 2) // 2, 0)
                group_v((step - 2) // 2, 1)
                invert_sums((step - 2) // 2)
            scores(step + 2)
            transpose_e(step - 1)
            if step in (PAIRS + 2, PAIRS + 3):
                keep_warm(12)
            if even:
                transpose_qk((step + 4) // 2)
            transpose_y(*divmod(step + 4, 2))
            if not even:
                attend(step - 5)
                attend(step - 4)
                project_values((step - 1) // 2, 0)
                project_values((step - 1) // 2, 1)
            if even:
                load_qky((step + 4) // 2 + 3)
                load("x", x, (step + 4) // 2, BATCHES)
